import numpy as np
import ml_dtypes


def mxq(x, axis, fmt="e4m3"):
    dtype, down = {"e4m3": (ml_dtypes.float8_e4m3fn, 7), "e5m2": (ml_dtypes.float8_e5m2, 14)}[fmt]
    v = np.moveaxis(np.asarray(x, np.float32).astype(ml_dtypes.bfloat16).astype(np.float64), axis, -1)
    blocks = v.reshape(v.shape[:-1] + (-1, 32))
    amax = np.abs(blocks).max(-1, keepdims=True)
    byte = np.maximum(np.where(amax > 0, np.frexp(amax)[1] - 1 + 127, 0) - down, 1)
    scale = np.exp2(byte - 127.0)
    codes = (blocks / scale).astype(np.float32).astype(dtype).astype(np.float64)
    return np.moveaxis((codes * scale).reshape(v.shape), -1, axis)


WIDE = False


def mx_kscale(k):
    if not WIDE:
        return np.ones(k)
    levels = np.array([10, -10, 5, -5, 0])
    a = np.random.permutation(np.resize(levels, k // 512 * 4)).reshape(k // 512, 4)
    idx = np.arange(k)
    return np.exp2(a[idx // 512, idx % 128 // 32])


BF16 = ml_dtypes.bfloat16


def bf(x):
    return np.asarray(x, np.float32).astype(BF16)


def f64(x):
    return np.asarray(x).astype(np.float64)


B, T, M, K, N, IN_MATS, OUT_MATS = 4, 1024, 4, 16, 32, 32, 8
KC = IN_MATS * K
WID = OUT_MATS * N
IN_FEATURES = IN_MATS * M * K
OUT_FEATURES = OUT_MATS * M * N


def setup_inputs():
    s = mx_kscale(KC).reshape(IN_MATS, 1, K)
    x = np.random.standard_normal((B, T, IN_MATS, M, K)) * s
    weight = np.random.standard_normal((OUT_MATS, IN_MATS, N, K)) / np.sqrt(KC) / s
    bias = np.random.standard_normal((OUT_MATS, M, N)) * 0.3
    return {"x": bf(x.reshape(B, T, IN_FEATURES)), "weight": bf(weight), "bias": bf(bias)}


def reference(x, weight, bias):
    Bc, Tc, _ = x.shape
    xb = f64(x).reshape(Bc, Tc, IN_MATS, M, K)
    xr = xb.transpose(0, 1, 3, 2, 4).reshape(Bc, Tc, M, KC)
    wr = f64(weight).transpose(0, 2, 1, 3).reshape(WID, KC)
    res = mxq(xr, 3, "e4m3") @ mxq(wr, 1, "e4m3").T
    res = res.reshape(Bc, Tc, M, OUT_MATS, N).transpose(0, 1, 3, 2, 4)
    res = res + f64(bias)
    return res.reshape(Bc, Tc, OUT_FEATURES)

@@ -1,0 +1,210 @@
+import concourse.mybir as mybir
+from concourse.masks import make_identity
+
+F32 = mybir.dt.float32
+BF16 = mybir.dt.bfloat16
+U32 = mybir.dt.uint32
+U8 = mybir.dt.uint8
+FP8X4 = mybir.dt.float8_e4m3fn_x4
+ADD = mybir.AluOpType.add
+
+P = 128
+FEAT = 2048
+OUTF = 1024
+TOKENS = 4096
+NT = TOKENS // P
+FLOPS = 2 * TOKENS * 4 * 512 * 256
+
+CHUNKS = [1, 1, 2, 4, 4, 4, 4, 4, 4, 2, 1, 1]
+X_BUFS = 5
+MANUAL = False
+STORE_Q = "gpsimd"
+
+
+def tile_blocklinear_t_kernel(tc, x, weight, bias, out):
+    nc = tc.nc
+    xf = x.flatten_outer_dims()
+    of = out.flatten_outer_dims()
+    assert sum(CHUNKS) == NT
+
+    where = []
+    bases = []
+    base = 0
+    for ci, a_cnt in enumerate(CHUNKS):
+        bases.append(base)
+        for a in range(a_cnt):
+            where.append((ci, a))
+        base += P * a_cnt
+
+    with tc.tile_pool(name="const", bufs=1) as const, \
+            tc.tile_pool(name="xin", bufs=X_BUFS) as xin, \
+            tc.tile_pool(name="work", bufs=3) as work, \
+            tc.tile_pool(name="res", bufs=5) as res, \
+            tc.psum_pool(name="ps", bufs=2) as ps:
+
+        x_tiles = {}
+
+        def load(ci):
+            a_cnt = CHUNKS[ci]
+            xt = xin.tile([P, a_cnt * FEAT], BF16, name="xchunk", tag="x")
+            rows = xf[bases[ci]:bases[ci] + P * a_cnt, :]
+            nc.sync.dma_start(out=xt[:], in_=rows.rearrange("(p a) f -> p (a f)", a=a_cnt))
+            x_tiles[ci] = xt
+
+        for ci in range(X_BUFS):
+            load(ci)
+
+        brow = const.tile([P, OUTF], BF16, name="brow")
+        nc.vector.memset(brow[:], 0.0)
+        ones = const.tile([P, P], BF16, name="ones")
+        nc.vector.memset(ones[:], 1.0)
+        w_sb = const.tile([P, 1024], BF16, name="w_sb")
+        for o in range(8):
+            nc.scalar.dma_start(
+                out=w_sb[o * 16:(o + 1) * 16, :].rearrange("p (c q) -> p c q", c=32),
+                in_=weight[o].rearrange("c (nh nl) k -> nh c (nl k)", nl=2),
+            )
+        nc.scalar.dma_start(out=brow[0:1, :], in_=bias.rearrange("(x o) m n -> x (o m n)", x=1))
+        ident = const.tile([P, P], F32, name="ident")
+        make_identity(nc, ident[:])
+
+        xp_tiles = {}
+        grp_tiles = {}
+        code_tiles = {}
+        acc_tiles = {}
+        out_tiles = {}
+
+        def permute(n):
+            ci, a = where[n]
+            src = x_tiles[ci]
+            xp = work.tile([P, FEAT], BF16, name="xp", tag="xp", bufs=4)
+            if n < 3 or n % 4 == 0:
+                nc.vector.tensor_copy(
+                    out=xp[:].rearrange("p (g i k) -> p g i k", g=8, i=16),
+                    in_=src[:, a * FEAT:(a + 1) * FEAT].rearrange("p (i g k) -> p g i k", g=8, i=16),
+                )
+            else:
+                nc.scalar.copy(
+                    out=xp[:].bitcast(F32).rearrange("p (g i k) -> p g i k", g=8, i=16),
+                    in_=src[:].bitcast(F32)[:, a * (FEAT // 2):(a + 1) * (FEAT // 2)].rearrange(
+                        "p (i g k) -> p g i k", g=8, i=16),
+                )
+            xp_tiles[n] = xp
+            if a == CHUNKS[ci] - 1 and ci + X_BUFS < len(CHUNKS):
+                load(ci + X_BUFS)
+
+        def transposes(n):
+            xpw = xp_tiles[n][:].bitcast(F32)
+            banks = []
+            for h in range(2):
+                bank = ps.tile([P, 2, 2, P], F32, name="xt%d" % h, tag="xt%d" % h)
+                for ml in range(2):
+                    for u in range(2):
+                        g = 4 * u + 2 * h + ml
+                        nc.tensor.transpose(bank[:, ml, u, :], xpw[:, g * P:(g + 1) * P], ident[:])
+                banks.append(bank)
+            return banks
+
+        def copy_out(n, banks):
+            grp = work.tile([P, FEAT], BF16, name="grp", tag="grp", align_bytes=64)
+            gw = grp[:].bitcast(F32)
+            for h in range(2):
+                nc.scalar.copy(
+                    out=gw[:, h * 512:(h + 1) * 512].rearrange("p (m r u) -> p m r u", m=2, u=2),
+                    in_=banks[h][:].rearrange("p m u r -> p m r u"),
+                )
+            grp_tiles[n] = grp
+
+        def quantise(n):
+            codes = work.tile([P, 512], U32, name="codes", tag="codes", align_bytes=64)
+            scl = work.tile([P, 512], U8, name="scl", tag="scl", align_bytes=64)
+            nc.vector.quantize_mx(out=codes[:].bitcast(FP8X4), scales=scl[:], in_=grp_tiles[n][:])
+            code_tiles[n] = (codes, scl)
+
+        def multiply(n):
+            codes, scl = code_tiles[n]
+            accs = []
+            for h in range(2):
+                acc = ps.tile([P, 512], F32, name="acc%d" % h, tag="acc%d" % h)
+                for ml in range(2):
+                    m = 2 * h + ml
+                    nc.tensor.matmul_mx(
+                        out=acc[:, ml * 256:(ml + 1) * 256],
+                        lhsT=codes[:, m * P:(m + 1) * P].bitcast(FP8X4),
+                        lhsT_scale=scl[:, m * P:(m + 1) * P],
+                        rhs=wcodes[:].bitcast(FP8X4),
+                        rhs_scale=wscl[:],
+                        start=True,
+                        stop=True,
+                    )
+                accs.append(acc)
+            acc_tiles[n] = accs
+
+        def add_bias_and_store(n):
+            ci, a = where[n]
+            a_cnt = CHUNKS[ci]
+            unit = min(2, a_cnt)
+            pos = a % unit
+            if pos == 0:
+                out_tiles[0] = res.tile([P, unit * OUTF], F32, name="osb", tag="osb")
+            osb = out_tiles[0]
+            dst = osb[:, pos * OUTF:(pos + 1) * OUTF].rearrange("p (o m n) -> p o m n", o=8, m=4)
+            bia = bias_sb[:].rearrange("p (o m n) -> p o m n", o=8, m=4)
+            for h in range(2):
+                nc.vector.tensor_tensor(
+                    out=dst[:, :, 2 * h:2 * h + 2, :],
+                    in0=acc_tiles[n][h][:].rearrange("p (m o n) -> p o m n", m=2, o=8),
+                    in1=bia[:, :, 2 * h:2 * h + 2, :],
+                    op=ADD,
+                )
+            if pos == unit - 1:
+                rows = of[bases[ci]:bases[ci] + P * a_cnt, :].rearrange("(p a) f -> p a f", a=a_cnt)
+                eng = nc.gpsimd if (STORE_Q == "gpsimd" and n < NT - 2) else nc.sync
+                eng.dma_start(
+                    out=rows[:, a - unit + 1:a + 1, :],
+                    in_=osb[:].rearrange("p (a f) -> p a f", a=unit),
+                )
+
+        permute(0)
+        banks0 = transposes(0)
+        copy_out(0, banks0)
+
+        wp = const.tile([P, 1024], BF16, name="wp")
+        nc.vector.tensor_copy(
+            out=wp[:].rearrange("p (g i k) -> p g i k", g=4, i=16),
+            in_=w_sb[:].rearrange("p (i g k) -> p g i k", g=4, i=16),
+        )
+        wpw = wp[:].bitcast(F32)
+        wt = ps.tile([P, 2, 2, P], F32, name="wt", tag="xt0")
+        for u in range(2):
+            for nl in range(2):
+                g = 2 * u + nl
+                nc.tensor.transpose(wt[:, nl, u, :], wpw[:, g * P:(g + 1) * P], ident[:])
+        wgrp = const.tile([P, 1024], BF16, name="wgrp", align_bytes=64)
+        nc.scalar.copy(
+            out=wgrp[:].bitcast(F32).rearrange("p (r nl u) -> p r nl u", nl=2, u=2),
+            in_=wt[:].rearrange("p nl u r -> p r nl u"),
+        )
+        wcodes = const.tile([P, 256], U32, name="wcodes", align_bytes=64)
+        wscl = const.tile([P, 256], U8, name="wscl", align_bytes=64)
+        permute(1)
+        nc.vector.quantize_mx(out=wcodes[:].bitcast(FP8X4), scales=wscl[:], in_=wgrp[:])
+
+        bias_sb = const.tile([P, OUTF], F32, name="bias_sb")
+        for h in range(2):
+            bp = ps.tile([P, 512], F32, name="bp%d" % h, tag="acc%d" % h)
+            nc.tensor.matmul(bp[:], lhsT=ones[:], rhs=brow[:, h * 512:(h + 1) * 512], start=True, stop=True)
+            nc.vector.tensor_copy(out=bias_sb[:, h * 512:(h + 1) * 512], in_=bp[:])
+        quantise(0)
+        permute(2)
+
+        for s in range(NT):
+            if s + 1 < NT:
+                banks = transposes(s + 1)
+                copy_out(s + 1, banks)
+            multiply(s)
+            if s + 1 < NT:
+                quantise(s + 1)
+            add_bias_and_store(s)
+            if s + 3 < NT:
+                permute(s + 3)

@@ -126,6 +126,16 @@ def tile_blocklinear_t_kernel(tc, x, weight, bias, out):
             accs = []
             for h in range(2):
                 acc = ps.tile([P, 512], F32, name="acc%d" % h, tag="acc%d" % h)
+                if h == 0:
+                    nc.tensor.matmul_mx(
+                        out=acc[:],
+                        lhsT=codes[:, 0:P].bitcast(FP8X4),
+                        lhsT_scale=scl[:, 0:P],
+                        rhs=codes[:].bitcast(FP8X4),
+                        rhs_scale=scl[:],
+                        start=True,
+                        stop=True,
+                    )
                 for ml in range(2):
                     m = 2 * h + ml
                     nc.tensor.matmul_mx(

@@ -16,9 +16,8 @@ NT = TOKENS // P
 FLOPS = 2 * TOKENS * 4 * 512 * 256
 
 CHUNKS = [1, 1, 2, 4, 4, 4, 4, 4, 4, 2, 1, 1]
-X_BUFS = 5
-MANUAL = False
-STORE_Q = "gpsimd"
+X_BUFS = 6
+V_EVERY = 4
 
 
 def tile_blocklinear_t_kernel(tc, x, weight, bias, out):
@@ -39,10 +38,17 @@ def tile_blocklinear_t_kernel(tc, x, weight, bias, out):
     with tc.tile_pool(name="const", bufs=1) as const, \
             tc.tile_pool(name="xin", bufs=X_BUFS) as xin, \
             tc.tile_pool(name="work", bufs=3) as work, \
-            tc.tile_pool(name="res", bufs=5) as res, \
-            tc.psum_pool(name="ps", bufs=2) as ps:
+            tc.tile_pool(name="res", bufs=6) as res, \
+            tc.psum_pool(name="ps", bufs=2) as ps, \
+            tc.manual_schedule():
 
         x_tiles = {}
+        xp_tiles = {}
+        bank_tiles = {}
+        grp_tiles = {}
+        code_tiles = {}
+        acc_tiles = {}
+        out_tiles = {}
 
         def load(ci):
             a_cnt = CHUNKS[ci]
@@ -51,34 +57,11 @@ def tile_blocklinear_t_kernel(tc, x, weight, bias, out):
             nc.sync.dma_start(out=xt[:], in_=rows.rearrange("(p a) f -> p (a f)", a=a_cnt))
             x_tiles[ci] = xt
 
-        for ci in range(X_BUFS):
-            load(ci)
-
-        brow = const.tile([P, OUTF], BF16, name="brow")
-        nc.vector.memset(brow[:], 0.0)
-        ones = const.tile([P, P], BF16, name="ones")
-        nc.vector.memset(ones[:], 1.0)
-        w_sb = const.tile([P, 1024], BF16, name="w_sb")
-        for o in range(8):
-            nc.scalar.dma_start(
-                out=w_sb[o * 16:(o + 1) * 16, :].rearrange("p (c q) -> p c q", c=32),
-                in_=weight[o].rearrange("c (nh nl) k -> nh c (nl k)", nl=2),
-            )
-        nc.scalar.dma_start(out=brow[0:1, :], in_=bias.rearrange("(x o) m n -> x (o m n)", x=1))
-        ident = const.tile([P, P], F32, name="ident")
-        make_identity(nc, ident[:])
-
-        xp_tiles = {}
-        grp_tiles = {}
-        code_tiles = {}
-        acc_tiles = {}
-        out_tiles = {}
-
-        def permute(n):
+        def permute(n, on_vector):
             ci, a = where[n]
             src = x_tiles[ci]
-            xp = work.tile([P, FEAT], BF16, name="xp", tag="xp", bufs=4)
-            if n < 3 or n % 4 == 0:
+            xp = work.tile([P, FEAT], BF16, name="xp", tag="xp", bufs=5)
+            if on_vector:
                 nc.vector.tensor_copy(
                     out=xp[:].rearrange("p (g i k) -> p g i k", g=8, i=16),
                     in_=src[:, a * FEAT:(a + 1) * FEAT].rearrange("p (i g k) -> p g i k", g=8, i=16),
@@ -103,15 +86,15 @@ def tile_blocklinear_t_kernel(tc, x, weight, bias, out):
                         g = 4 * u + 2 * h + ml
                         nc.tensor.transpose(bank[:, ml, u, :], xpw[:, g * P:(g + 1) * P], ident[:])
                 banks.append(bank)
-            return banks
+            bank_tiles[n] = banks
 
-        def copy_out(n, banks):
+        def copy_out(n):
             grp = work.tile([P, FEAT], BF16, name="grp", tag="grp", align_bytes=64)
             gw = grp[:].bitcast(F32)
             for h in range(2):
                 nc.scalar.copy(
                     out=gw[:, h * 512:(h + 1) * 512].rearrange("p (m r u) -> p m r u", m=2, u=2),
-                    in_=banks[h][:].rearrange("p m u r -> p m r u"),
+                    in_=bank_tiles[n][h][:].rearrange("p m u r -> p m r u"),
                 )
             grp_tiles[n] = grp
 
@@ -126,16 +109,6 @@ def tile_blocklinear_t_kernel(tc, x, weight, bias, out):
             accs = []
             for h in range(2):
                 acc = ps.tile([P, 512], F32, name="acc%d" % h, tag="acc%d" % h)
-                if h == 0:
-                    nc.tensor.matmul_mx(
-                        out=acc[:],
-                        lhsT=codes[:, 0:P].bitcast(FP8X4),
-                        lhsT_scale=scl[:, 0:P],
-                        rhs=codes[:].bitcast(FP8X4),
-                        rhs_scale=scl[:],
-                        start=True,
-                        stop=True,
-                    )
                 for ml in range(2):
                     m = 2 * h + ml
                     nc.tensor.matmul_mx(
@@ -169,15 +142,37 @@ def tile_blocklinear_t_kernel(tc, x, weight, bias, out):
                 )
             if pos == unit - 1:
                 rows = of[bases[ci]:bases[ci] + P * a_cnt, :].rearrange("(p a) f -> p a f", a=a_cnt)
-                eng = nc.gpsimd if (STORE_Q == "gpsimd" and n < NT - 2) else nc.sync
+                eng = nc.gpsimd if n < NT - 2 else nc.sync
                 eng.dma_start(
                     out=rows[:, a - unit + 1:a + 1, :],
                     in_=osb[:].rearrange("p (a f) -> p a f", a=unit),
                 )
 
-        permute(0)
-        banks0 = transposes(0)
-        copy_out(0, banks0)
+        brow = const.tile([P, OUTF], BF16, name="brow")
+        nc.vector.memset(brow[:], 0.0)
+        ones = const.tile([P, P], BF16, name="ones")
+        nc.vector.memset(ones[:], 1.0)
+        w_sb = const.tile([P, 1024], BF16, name="w_sb")
+
+        def load_w(eng, o):
+            eng.dma_start(
+                out=w_sb[o * 16:(o + 1) * 16, :].rearrange("p (c q) -> p c q", c=32),
+                in_=weight[o].rearrange("c (nh nl) k -> nh c (nl k)", nl=2),
+            )
+
+        for o in range(7):
+            load_w(nc.scalar, o)
+        load(0)
+        load_w(nc.sync, 7)
+        nc.sync.dma_start(out=brow[0:1, :], in_=bias.rearrange("(x o) m n -> x (o m n)", x=1))
+        ident = const.tile([P, P], F32, name="ident")
+        make_identity(nc, ident[:])
+        for ci in range(1, X_BUFS):
+            load(ci)
+
+        permute(0, True)
+        transposes(0)
+        copy_out(0)
 
         wp = const.tile([P, 1024], BF16, name="wp")
         nc.vector.tensor_copy(
@@ -197,24 +192,28 @@ def tile_blocklinear_t_kernel(tc, x, weight, bias, out):
         )
         wcodes = const.tile([P, 256], U32, name="wcodes", align_bytes=64)
         wscl = const.tile([P, 256], U8, name="wscl", align_bytes=64)
-        permute(1)
+        permute(1, True)
+        transposes(1)
+        quantise(0)
         nc.vector.quantize_mx(out=wcodes[:].bitcast(FP8X4), scales=wscl[:], in_=wgrp[:])
-
+        copy_out(1)
         bias_sb = const.tile([P, OUTF], F32, name="bias_sb")
         for h in range(2):
             bp = ps.tile([P, 512], F32, name="bp%d" % h, tag="acc%d" % h)
             nc.tensor.matmul(bp[:], lhsT=ones[:], rhs=brow[:, h * 512:(h + 1) * 512], start=True, stop=True)
-            nc.vector.tensor_copy(out=bias_sb[:, h * 512:(h + 1) * 512], in_=bp[:])
-        quantise(0)
-        permute(2)
+            nc.scalar.copy(out=bias_sb[:, h * 512:(h + 1) * 512], in_=bp[:])
+        permute(2, True)
+        permute(3, True)
 
-        for s in range(NT):
-            if s + 1 < NT:
-                banks = transposes(s + 1)
-                copy_out(s + 1, banks)
-            multiply(s)
+        for s in range(NT + 1):
+            if s + 4 < NT:
+                permute(s + 4, (s + 4) % V_EVERY == 0)
+            if s + 2 < NT:
+                transposes(s + 2)
+                copy_out(s + 2)
+            if s >= 1:
+                add_bias_and_store(s - 1)
+            if s < NT:
+                multiply(s)
             if s + 1 < NT:
                 quantise(s + 1)
-            add_bias_and_store(s)
-            if s + 3 < NT:
-                permute(s + 3)

@@ -15,8 +15,8 @@ TOKENS = 4096
 NT = TOKENS // P
 FLOPS = 2 * TOKENS * 4 * 512 * 256
 
-CHUNKS = [1, 1, 2, 4, 4, 4, 4, 4, 4, 2, 1, 1]
-X_BUFS = 6
+CHUNKS = [1, 1, 1, 1, 2, 2, 4, 4, 4, 4, 4, 2, 1, 1]
+X_SLOTS = {1: 4, 2: 2, 4: 5}
 V_EVERY = 4
 
 
@@ -36,7 +36,7 @@ def tile_blocklinear_t_kernel(tc, x, weight, bias, out):
         base += P * a_cnt
 
     with tc.tile_pool(name="const", bufs=1) as const, \
-            tc.tile_pool(name="xin", bufs=X_BUFS) as xin, \
+            tc.tile_pool(name="xin", bufs=1) as xin, \
             tc.tile_pool(name="work", bufs=3) as work, \
             tc.tile_pool(name="res", bufs=6) as res, \
             tc.psum_pool(name="ps", bufs=2) as ps, \
@@ -52,7 +52,7 @@ def tile_blocklinear_t_kernel(tc, x, weight, bias, out):
 
         def load(ci):
             a_cnt = CHUNKS[ci]
-            xt = xin.tile([P, a_cnt * FEAT], BF16, name="xchunk", tag="x")
+            xt = xin.tile([P, a_cnt * FEAT], BF16, name="xchunk", tag="x%d" % a_cnt, bufs=X_SLOTS[a_cnt])
             rows = xf[bases[ci]:bases[ci] + P * a_cnt, :]
             nc.sync.dma_start(out=xt[:], in_=rows.rearrange("(p a) f -> p (a f)", a=a_cnt))
             x_tiles[ci] = xt
@@ -60,7 +60,7 @@ def tile_blocklinear_t_kernel(tc, x, weight, bias, out):
         def permute(n, on_vector):
             ci, a = where[n]
             src = x_tiles[ci]
-            xp = work.tile([P, FEAT], BF16, name="xp", tag="xp", bufs=5)
+            xp = work.tile([P, FEAT], BF16, name="xp", tag="xp", bufs=4)
             if on_vector:
                 nc.vector.tensor_copy(
                     out=xp[:].rearrange("p (g i k) -> p g i k", g=8, i=16),
@@ -73,8 +73,6 @@ def tile_blocklinear_t_kernel(tc, x, weight, bias, out):
                         "p (i g k) -> p g i k", g=8, i=16),
                 )
             xp_tiles[n] = xp
-            if a == CHUNKS[ci] - 1 and ci + X_BUFS < len(CHUNKS):
-                load(ci + X_BUFS)
 
         def transposes(n):
             xpw = xp_tiles[n][:].bitcast(F32)
@@ -167,12 +165,14 @@ def tile_blocklinear_t_kernel(tc, x, weight, bias, out):
         nc.sync.dma_start(out=brow[0:1, :], in_=bias.rearrange("(x o) m n -> x (o m n)", x=1))
         ident = const.tile([P, P], F32, name="ident")
         make_identity(nc, ident[:])
-        for ci in range(1, X_BUFS):
+        for ci in range(1, len(CHUNKS)):
             load(ci)
 
         permute(0, True)
         transposes(0)
         copy_out(0)
+        permute(1, True)
+        transposes(1)
 
         wp = const.tile([P, 1024], BF16, name="wp")
         nc.vector.tensor_copy(
@@ -180,7 +180,7 @@ def tile_blocklinear_t_kernel(tc, x, weight, bias, out):
             in_=w_sb[:].rearrange("p (i g k) -> p g i k", g=4, i=16),
         )
         wpw = wp[:].bitcast(F32)
-        wt = ps.tile([P, 2, 2, P], F32, name="wt", tag="xt0")
+        wt = ps.tile([P, 2, 2, P], F32, name="wt", tag="acc0")
         for u in range(2):
             for nl in range(2):
                 g = 2 * u + nl
@@ -192,22 +192,19 @@ def tile_blocklinear_t_kernel(tc, x, weight, bias, out):
         )
         wcodes = const.tile([P, 256], U32, name="wcodes", align_bytes=64)
         wscl = const.tile([P, 256], U8, name="wscl", align_bytes=64)
-        permute(1, True)
-        transposes(1)
+        copy_out(1)
+        permute(2, True)
         quantise(0)
         nc.vector.quantize_mx(out=wcodes[:].bitcast(FP8X4), scales=wscl[:], in_=wgrp[:])
-        copy_out(1)
         bias_sb = const.tile([P, OUTF], F32, name="bias_sb")
         for h in range(2):
-            bp = ps.tile([P, 512], F32, name="bp%d" % h, tag="acc%d" % h)
+            bp = ps.tile([P, 512], F32, name="bp%d" % h, tag="acc%d" % (1 - h))
             nc.tensor.matmul(bp[:], lhsT=ones[:], rhs=brow[:, h * 512:(h + 1) * 512], start=True, stop=True)
             nc.scalar.copy(out=bias_sb[:, h * 512:(h + 1) * 512], in_=bp[:])
-        permute(2, True)
-        permute(3, True)
 
         for s in range(NT + 1):
-            if s + 4 < NT:
-                permute(s + 4, (s + 4) % V_EVERY == 0)
+            if s + 3 < NT:
+                permute(s + 3, (s + 3) % V_EVERY == 0 or s == 0)
             if s + 2 < NT:
                 transposes(s + 2)
                 copy_out(s + 2)

@@ -17,7 +17,7 @@ FLOPS = 2 * TOKENS * 4 * 512 * 256
 
 CHUNKS = [1, 1, 1, 1, 2, 2, 4, 4, 4, 4, 4, 2, 1, 1]
 X_SLOTS = {1: 4, 2: 2, 4: 5}
-V_EVERY = 4
+V_EVERY = 2
 
 
 def tile_blocklinear_t_kernel(tc, x, weight, bias, out):

@@ -17,7 +17,7 @@ FLOPS = 2 * TOKENS * 4 * 512 * 256
 
 CHUNKS = [1, 1, 1, 1, 2, 2, 4, 4, 4, 4, 4, 2, 1, 1]
 X_SLOTS = {1: 4, 2: 2, 4: 5}
-V_EVERY = 2
+V_TILES = (0, 1, 2, 3, 4, 7, 10, 13, 16, 19, 22)
 
 
 def tile_blocklinear_t_kernel(tc, x, weight, bias, out):
@@ -158,15 +158,22 @@ def tile_blocklinear_t_kernel(tc, x, weight, bias, out):
                 in_=weight[o].rearrange("c (nh nl) k -> nh c (nl k)", nl=2),
             )
 
-        for o in range(7):
+        for o in range(6):
             load_w(nc.scalar, o)
+        nc.scalar.dma_start(out=brow[0:1, :], in_=bias.rearrange("(x o) m n -> x (o m n)", x=1))
         load(0)
+        load_w(nc.sync, 6)
         load_w(nc.sync, 7)
-        nc.sync.dma_start(out=brow[0:1, :], in_=bias.rearrange("(x o) m n -> x (o m n)", x=1))
         ident = const.tile([P, P], F32, name="ident")
         make_identity(nc, ident[:])
         for ci in range(1, len(CHUNKS)):
             load(ci)
+
+        bias_sb = const.tile([P, OUTF], F32, name="bias_sb")
+        for h in range(2):
+            bp = ps.tile([P, 512], F32, name="bp%d" % h, tag="acc%d" % (1 - h))
+            nc.tensor.matmul(bp[:], lhsT=ones[:], rhs=brow[:, h * 512:(h + 1) * 512], start=True, stop=True)
+            nc.scalar.copy(out=bias_sb[:, h * 512:(h + 1) * 512], in_=bp[:])
 
         permute(0, True)
         transposes(0)
@@ -196,15 +203,10 @@ def tile_blocklinear_t_kernel(tc, x, weight, bias, out):
         permute(2, True)
         quantise(0)
         nc.vector.quantize_mx(out=wcodes[:].bitcast(FP8X4), scales=wscl[:], in_=wgrp[:])
-        bias_sb = const.tile([P, OUTF], F32, name="bias_sb")
-        for h in range(2):
-            bp = ps.tile([P, 512], F32, name="bp%d" % h, tag="acc%d" % (1 - h))
-            nc.tensor.matmul(bp[:], lhsT=ones[:], rhs=brow[:, h * 512:(h + 1) * 512], start=True, stop=True)
-            nc.scalar.copy(out=bias_sb[:, h * 512:(h + 1) * 512], in_=bp[:])
 
         for s in range(NT + 1):
             if s + 3 < NT:
-                permute(s + 3, (s + 3) % V_EVERY == 0 or s == 0)
+                permute(s + 3, (s + 3) in V_TILES)
             if s + 2 < NT:
                 transposes(s + 2)
                 copy_out(s + 2)

@@ -17,7 +17,7 @@ FLOPS = 2 * TOKENS * 4 * 512 * 256
 
 CHUNKS = [1, 1, 1, 1, 2, 2, 4, 4, 4, 4, 4, 2, 1, 1]
 X_SLOTS = {1: 4, 2: 2, 4: 5}
-V_TILES = (0, 1, 2, 3, 4, 7, 10, 13, 16, 19, 22)
+V_EVERY = 4
 
 
 def tile_blocklinear_t_kernel(tc, x, weight, bias, out):
@@ -150,63 +150,64 @@ def tile_blocklinear_t_kernel(tc, x, weight, bias, out):
         nc.vector.memset(brow[:], 0.0)
         ones = const.tile([P, P], BF16, name="ones")
         nc.vector.memset(ones[:], 1.0)
-        w_sb = const.tile([P, 1024], BF16, name="w_sb")
-
-        def load_w(eng, o):
-            eng.dma_start(
-                out=w_sb[o * 16:(o + 1) * 16, :].rearrange("p (c q) -> p c q", c=32),
-                in_=weight[o].rearrange("c (nh nl) k -> nh c (nl k)", nl=2),
-            )
-
-        for o in range(6):
-            load_w(nc.scalar, o)
-        nc.scalar.dma_start(out=brow[0:1, :], in_=bias.rearrange("(x o) m n -> x (o m n)", x=1))
+        wa = const.tile([P, 1024], BF16, name="wa")
+        nc.sync.dma_start(
+            out=wa[:].rearrange("p (ol q) -> p ol q", ol=2),
+            in_=weight.rearrange("(ol oh) c n k -> (oh c) ol (n k)", ol=2),
+        )
         load(0)
-        load_w(nc.sync, 6)
-        load_w(nc.sync, 7)
-        ident = const.tile([P, P], F32, name="ident")
-        make_identity(nc, ident[:])
+        nc.sync.dma_start(out=brow[0:1, :], in_=bias.rearrange("(x o) m n -> x (o m n)", x=1))
         for ci in range(1, len(CHUNKS)):
             load(ci)
+        identb = const.tile([P, P], BF16, name="identb")
+        make_identity(nc, identb[:])
+        ident = const.tile([P, P], F32, name="ident")
+        make_identity(nc, ident[:])
 
-        bias_sb = const.tile([P, OUTF], F32, name="bias_sb")
-        for h in range(2):
-            bp = ps.tile([P, 512], F32, name="bp%d" % h, tag="acc%d" % (1 - h))
-            nc.tensor.matmul(bp[:], lhsT=ones[:], rhs=brow[:, h * 512:(h + 1) * 512], start=True, stop=True)
-            nc.scalar.copy(out=bias_sb[:, h * 512:(h + 1) * 512], in_=bp[:])
+        wb = const.tile([P, 1024], BF16, name="wb")
+        nc.vector.tensor_copy(
+            out=wb[:].bitcast(F32).rearrange("p (k q) -> p k q", k=8),
+            in_=wa[:].bitcast(F32).rearrange("p (q k) -> p k q", k=8),
+        )
+        y_ps = ps.tile([P, 1024], BF16, name="y_ps", tag="acc0")
+        for k2 in range(8):
+            nc.tensor.transpose(y_ps[:, k2 * P:(k2 + 1) * P], wb[:, k2 * P:(k2 + 1) * P], identb[:])
+        y_sb = const.tile([P, 1024], BF16, name="y_sb")
+        ysv = y_sb[:].rearrange("p (oh u i k) -> p u oh i k", oh=4, u=2, i=16)
+        ypv = y_ps[:].rearrange("p (k oh i u) -> p u oh i k", k=8, oh=4, i=16)
+        for u in range(2):
+            nc.scalar.copy(out=ysv[:, u], in_=ypv[:, u])
 
         permute(0, True)
         transposes(0)
         copy_out(0)
-        permute(1, True)
-        transposes(1)
 
-        wp = const.tile([P, 1024], BF16, name="wp")
-        nc.vector.tensor_copy(
-            out=wp[:].rearrange("p (g i k) -> p g i k", g=4, i=16),
-            in_=w_sb[:].rearrange("p (i g k) -> p g i k", g=4, i=16),
-        )
-        wpw = wp[:].bitcast(F32)
-        wt = ps.tile([P, 2, 2, P], F32, name="wt", tag="acc0")
-        for u in range(2):
-            for nl in range(2):
-                g = 2 * u + nl
-                nc.tensor.transpose(wt[:, nl, u, :], wpw[:, g * P:(g + 1) * P], ident[:])
+        z_ps = ps.tile([P, 1024], BF16, name="z_ps", tag="acc1")
+        for q in range(8):
+            nc.tensor.transpose(z_ps[:, q * P:(q + 1) * P], y_sb[:, q * P:(q + 1) * P], identb[:])
         wgrp = const.tile([P, 1024], BF16, name="wgrp", align_bytes=64)
-        nc.scalar.copy(
-            out=wgrp[:].bitcast(F32).rearrange("p (r nl u) -> p r nl u", nl=2, u=2),
-            in_=wt[:].rearrange("p nl u r -> p r nl u"),
-        )
+        wgv = wgrp[:].bitcast(F32).rearrange("p (ol oh n u) -> p ol oh n u", ol=2, oh=4, u=2)
+        zv = z_ps[:].bitcast(F32).rearrange("p (oh u ol n) -> p ol oh n u", oh=4, u=2, ol=2)
+        for ol in range(2):
+            nc.scalar.copy(out=wgv[:, ol], in_=zv[:, ol])
         wcodes = const.tile([P, 256], U32, name="wcodes", align_bytes=64)
         wscl = const.tile([P, 256], U8, name="wscl", align_bytes=64)
-        copy_out(1)
+
+        permute(1, True)
+        transposes(1)
         permute(2, True)
-        quantise(0)
         nc.vector.quantize_mx(out=wcodes[:].bitcast(FP8X4), scales=wscl[:], in_=wgrp[:])
+        copy_out(1)
+        quantise(0)
+        bias_sb = const.tile([P, OUTF], F32, name="bias_sb")
+        for h in range(2):
+            bp = ps.tile([P, 512], F32, name="bp%d" % h, tag="acc%d" % h)
+            nc.tensor.matmul(bp[:], lhsT=ones[:], rhs=brow[:, h * 512:(h + 1) * 512], start=True, stop=True)
+            nc.scalar.copy(out=bias_sb[:, h * 512:(h + 1) * 512], in_=bp[:])
 
         for s in range(NT + 1):
             if s + 3 < NT:
-                permute(s + 3, (s + 3) in V_TILES)
+                permute(s + 3, (s + 3) % V_EVERY == 0 or s == 0)
             if s + 2 < NT:
                 transposes(s + 2)
                 copy_out(s + 2)

@@ -15,7 +15,7 @@ TOKENS = 4096
 NT = TOKENS // P
 FLOPS = 2 * TOKENS * 4 * 512 * 256
 
-CHUNKS = [1, 1, 1, 1, 2, 2, 4, 4, 4, 4, 4, 2, 1, 1]
+CHUNKS = [1, 1, 1, 1, 2, 2, 4, 4, 4, 4, 4, 1, 1, 1, 1]
 X_SLOTS = {1: 4, 2: 2, 4: 5}
 V_EVERY = 4
 
@@ -107,14 +107,13 @@ def tile_blocklinear_t_kernel(tc, x, weight, bias, out):
             accs = []
             for h in range(2):
                 acc = ps.tile([P, 512], F32, name="acc%d" % h, tag="acc%d" % h)
-                for ml in range(2):
-                    m = 2 * h + ml
+                for m in range(4):
                     nc.tensor.matmul_mx(
-                        out=acc[:, ml * 256:(ml + 1) * 256],
+                        out=acc[:, m * P:(m + 1) * P],
                         lhsT=codes[:, m * P:(m + 1) * P].bitcast(FP8X4),
                         lhsT_scale=scl[:, m * P:(m + 1) * P],
-                        rhs=wcodes[:].bitcast(FP8X4),
-                        rhs_scale=wscl[:],
+                        rhs=wcodes[:, h * P:(h + 1) * P].bitcast(FP8X4),
+                        rhs_scale=wscl[:, h * P:(h + 1) * P],
                         start=True,
                         stop=True,
                     )
@@ -129,17 +128,18 @@ def tile_blocklinear_t_kernel(tc, x, weight, bias, out):
             if pos == 0:
                 out_tiles[0] = res.tile([P, unit * OUTF], F32, name="osb", tag="osb")
             osb = out_tiles[0]
-            dst = osb[:, pos * OUTF:(pos + 1) * OUTF].rearrange("p (o m n) -> p o m n", o=8, m=4)
-            bia = bias_sb[:].rearrange("p (o m n) -> p o m n", o=8, m=4)
+            rows = of[bases[ci]:bases[ci] + P * a_cnt, :].rearrange("(p a) f -> p a f", a=a_cnt)
             for h in range(2):
+                lo = pos * OUTF + h * 512
                 nc.vector.tensor_tensor(
-                    out=dst[:, :, 2 * h:2 * h + 2, :],
-                    in0=acc_tiles[n][h][:].rearrange("p (m o n) -> p o m n", m=2, o=8),
-                    in1=bia[:, :, 2 * h:2 * h + 2, :],
+                    out=osb[:, lo:lo + 512].rearrange("p (o m n) -> p o m n", o=4, m=4),
+                    in0=acc_tiles[n][h][:].rearrange("p (m o n) -> p o m n", m=4, o=4),
+                    in1=bias_sb[:, h * 512:(h + 1) * 512].rearrange("p (o m n) -> p o m n", o=4, m=4),
                     op=ADD,
                 )
-            if pos == unit - 1:
-                rows = of[bases[ci]:bases[ci] + P * a_cnt, :].rearrange("(p a) f -> p a f", a=a_cnt)
+                if n == NT - 1:
+                    nc.sync.dma_start(out=rows[:, a, h * 512:(h + 1) * 512], in_=osb[:, lo:lo + 512])
+            if pos == unit - 1 and n < NT - 1:
                 eng = nc.gpsimd if n < NT - 2 else nc.sync
                 eng.dma_start(
                     out=rows[:, a - unit + 1:a + 1, :],

@@ -18,6 +18,8 @@ FLOPS = 2 * TOKENS * 4 * 512 * 256
 CHUNKS = [1, 1, 1, 1, 2, 2, 4, 4, 4, 4, 4, 1, 1, 1, 1]
 X_SLOTS = {1: 4, 2: 2, 4: 5}
 V_EVERY = 4
+HEAD_TILES = 12
+AHEAD = 10
 
 
 def tile_blocklinear_t_kernel(tc, x, weight, bias, out):
@@ -140,8 +142,7 @@ def tile_blocklinear_t_kernel(tc, x, weight, bias, out):
                 if n == NT - 1:
                     nc.sync.dma_start(out=rows[:, a, h * 512:(h + 1) * 512], in_=osb[:, lo:lo + 512])
             if pos == unit - 1 and n < NT - 1:
-                eng = nc.gpsimd if n < NT - 2 else nc.sync
-                eng.dma_start(
+                nc.sync.dma_start(
                     out=rows[:, a - unit + 1:a + 1, :],
                     in_=osb[:].rearrange("p (a f) -> p a f", a=unit),
                 )
@@ -158,7 +159,8 @@ def tile_blocklinear_t_kernel(tc, x, weight, bias, out):
         load(0)
         nc.sync.dma_start(out=brow[0:1, :], in_=bias.rearrange("(x o) m n -> x (o m n)", x=1))
         for ci in range(1, len(CHUNKS)):
-            load(ci)
+            if bases[ci] < HEAD_TILES * P:
+                load(ci)
         identb = const.tile([P, P], BF16, name="identb")
         make_identity(nc, identb[:])
         ident = const.tile([P, P], F32, name="ident")
@@ -206,6 +208,9 @@ def tile_blocklinear_t_kernel(tc, x, weight, bias, out):
             nc.scalar.copy(out=bias_sb[:, h * 512:(h + 1) * 512], in_=bp[:])
 
         for s in range(NT + 1):
+            for ci in range(len(CHUNKS)):
+                if bases[ci] >= HEAD_TILES * P and max(bases[ci] // P - AHEAD, 0) == s:
+                    load(ci)
             if s + 3 < NT:
                 permute(s + 3, (s + 3) % V_EVERY == 0 or s == 0)
             if s + 2 < NT:

@@ -19,6 +19,8 @@ CHUNKS = [1, 1, 1, 1, 2, 2, 4, 4, 4, 4, 4, 1, 1, 1, 1]
 X_SLOTS = {1: 4, 2: 2, 4: 5}
 V_EVERY = 4
 HEAD_TILES = 12
+G_AHEAD = 6
+G_PIECES = 4
 AHEAD = 10
 
 
@@ -58,6 +60,17 @@ def tile_blocklinear_t_kernel(tc, x, weight, bias, out):
             rows = xf[bases[ci]:bases[ci] + P * a_cnt, :]
             nc.sync.dma_start(out=xt[:], in_=rows.rearrange("(p a) f -> p (a f)", a=a_cnt))
             x_tiles[ci] = xt
+
+        def permute_gpsimd(n):
+            ci, a = where[n]
+            xp = work.tile([P, FEAT], BF16, name="xpg", tag="xpg", bufs=2)
+            words = x_tiles[ci][:].bitcast(F32)[:, a * (FEAT // 2):(a + 1) * (FEAT // 2)].rearrange(
+                "p (i g k) -> p g i k", g=8, i=16)
+            sorted_words = xp[:].bitcast(F32).rearrange("p (g i k) -> p g i k", g=8, i=16)
+            per = 8 // G_PIECES
+            for q in range(G_PIECES):
+                nc.gpsimd.tensor_copy(out=sorted_words[:, q * per:(q + 1) * per], in_=words[:, q * per:(q + 1) * per])
+            xp_tiles[n] = xp
 
         def permute(n, on_vector):
             ci, a = where[n]
@@ -211,7 +224,9 @@ def tile_blocklinear_t_kernel(tc, x, weight, bias, out):
             for ci in range(len(CHUNKS)):
                 if bases[ci] >= HEAD_TILES * P and max(bases[ci] // P - AHEAD, 0) == s:
                     load(ci)
-            if s + 3 < NT:
+            if s + G_AHEAD < NT and (s + G_AHEAD) % V_EVERY == 0:
+                permute_gpsimd(s + G_AHEAD)
+            if s + 3 < NT and ((s + 3) % V_EVERY != 0 or s + 3 < G_AHEAD):
                 permute(s + 3, (s + 3) % V_EVERY == 0 or s == 0)
             if s + 2 < NT:
                 transposes(s + 2)

@@ -17,7 +17,7 @@ FLOPS = 2 * TOKENS * 4 * 512 * 256
 
 CHUNKS = [1, 1, 1, 1, 2, 2, 4, 4, 4, 4, 4, 1, 1, 1, 1]
 X_SLOTS = {1: 4, 2: 2, 4: 5}
-V_EVERY = 4
+G_EVERY = 2
 HEAD_TILES = 12
 G_AHEAD = 6
 G_PIECES = 4
@@ -63,7 +63,7 @@ def tile_blocklinear_t_kernel(tc, x, weight, bias, out):
 
         def permute_gpsimd(n):
             ci, a = where[n]
-            xp = work.tile([P, FEAT], BF16, name="xpg", tag="xpg", bufs=2)
+            xp = work.tile([P, FEAT], BF16, name="xpg", tag="xpg", bufs=3)
             words = x_tiles[ci][:].bitcast(F32)[:, a * (FEAT // 2):(a + 1) * (FEAT // 2)].rearrange(
                 "p (i g k) -> p g i k", g=8, i=16)
             sorted_words = xp[:].bitcast(F32).rearrange("p (g i k) -> p g i k", g=8, i=16)
@@ -224,10 +224,10 @@ def tile_blocklinear_t_kernel(tc, x, weight, bias, out):
             for ci in range(len(CHUNKS)):
                 if bases[ci] >= HEAD_TILES * P and max(bases[ci] // P - AHEAD, 0) == s:
                     load(ci)
-            if s + G_AHEAD < NT and (s + G_AHEAD) % V_EVERY == 0:
+            if s + G_AHEAD < NT and s + G_AHEAD >= 8 and (s + G_AHEAD) % G_EVERY == 0:
                 permute_gpsimd(s + G_AHEAD)
-            if s + 3 < NT and ((s + 3) % V_EVERY != 0 or s + 3 < G_AHEAD):
-                permute(s + 3, (s + 3) % V_EVERY == 0 or s == 0)
+            if s + 3 < NT and ((s + 3) % G_EVERY != 0 or s + 3 < 8):
+                permute(s + 3, s + 3 in (3, 4))
             if s + 2 < NT:
                 transposes(s + 2)
                 copy_out(s + 2)

@@ -15,20 +15,18 @@ TOKENS = 4096
 NT = TOKENS // P
 FLOPS = 2 * TOKENS * 4 * 512 * 256
 
-CHUNKS = [1, 1, 1, 1, 2, 2, 4, 4, 4, 4, 4, 1, 1, 1, 1]
-X_SLOTS = {1: 4, 2: 2, 4: 5}
+CHUNKS = [1, 1, 2, 4, 6, 8, 10]
+UNITS = [1, 1, 2, 4, 6, 8, 4, 3, 2, 1]
 G_EVERY = 2
-HEAD_TILES = 12
 G_AHEAD = 6
 G_PIECES = 4
-AHEAD = 10
 
 
 def tile_blocklinear_t_kernel(tc, x, weight, bias, out):
     nc = tc.nc
     xf = x.flatten_outer_dims()
     of = out.flatten_outer_dims()
-    assert sum(CHUNKS) == NT
+    assert sum(CHUNKS) == NT and sum(UNITS) == NT
 
     where = []
     bases = []
@@ -38,11 +36,16 @@ def tile_blocklinear_t_kernel(tc, x, weight, bias, out):
         for a in range(a_cnt):
             where.append((ci, a))
         base += P * a_cnt
+    unit_of_last = {}
+    first = 0
+    for cnt in UNITS:
+        assert where[first][0] == where[first + cnt - 1][0]
+        unit_of_last[first + cnt - 1] = cnt
+        first += cnt
 
     with tc.tile_pool(name="const", bufs=1) as const, \
             tc.tile_pool(name="xin", bufs=1) as xin, \
             tc.tile_pool(name="work", bufs=3) as work, \
-            tc.tile_pool(name="res", bufs=6) as res, \
             tc.psum_pool(name="ps", bufs=2) as ps, \
             tc.manual_schedule():
 
@@ -52,11 +55,10 @@ def tile_blocklinear_t_kernel(tc, x, weight, bias, out):
         grp_tiles = {}
         code_tiles = {}
         acc_tiles = {}
-        out_tiles = {}
 
         def load(ci):
             a_cnt = CHUNKS[ci]
-            xt = xin.tile([P, a_cnt * FEAT], BF16, name="xchunk", tag="x%d" % a_cnt, bufs=X_SLOTS[a_cnt])
+            xt = xin.tile([P, a_cnt * FEAT], BF16, name="xchunk", tag="x%d" % ci)
             rows = xf[bases[ci]:bases[ci] + P * a_cnt, :]
             nc.sync.dma_start(out=xt[:], in_=rows.rearrange("(p a) f -> p (a f)", a=a_cnt))
             x_tiles[ci] = xt
@@ -138,14 +140,10 @@ def tile_blocklinear_t_kernel(tc, x, weight, bias, out):
         def add_bias_and_store(n):
             ci, a = where[n]
             a_cnt = CHUNKS[ci]
-            unit = min(2, a_cnt)
-            pos = a % unit
-            if pos == 0:
-                out_tiles[0] = res.tile([P, unit * OUTF], F32, name="osb", tag="osb")
-            osb = out_tiles[0]
+            osb = x_tiles[ci][:].bitcast(F32)
             rows = of[bases[ci]:bases[ci] + P * a_cnt, :].rearrange("(p a) f -> p a f", a=a_cnt)
             for h in range(2):
-                lo = pos * OUTF + h * 512
+                lo = a * OUTF + h * 512
                 nc.vector.tensor_tensor(
                     out=osb[:, lo:lo + 512].rearrange("p (o m n) -> p o m n", o=4, m=4),
                     in0=acc_tiles[n][h][:].rearrange("p (m o n) -> p o m n", m=4, o=4),
@@ -154,10 +152,11 @@ def tile_blocklinear_t_kernel(tc, x, weight, bias, out):
                 )
                 if n == NT - 1:
                     nc.sync.dma_start(out=rows[:, a, h * 512:(h + 1) * 512], in_=osb[:, lo:lo + 512])
-            if pos == unit - 1 and n < NT - 1:
+            if n in unit_of_last and n < NT - 1:
+                cnt = unit_of_last[n]
                 nc.sync.dma_start(
-                    out=rows[:, a - unit + 1:a + 1, :],
-                    in_=osb[:].rearrange("p (a f) -> p a f", a=unit),
+                    out=rows[:, a - cnt + 1:a + 1, :],
+                    in_=osb[:, (a - cnt + 1) * OUTF:(a + 1) * OUTF].rearrange("p (a f) -> p a f", a=cnt),
                 )
 
         brow = const.tile([P, OUTF], BF16, name="brow")
@@ -172,8 +171,7 @@ def tile_blocklinear_t_kernel(tc, x, weight, bias, out):
         load(0)
         nc.sync.dma_start(out=brow[0:1, :], in_=bias.rearrange("(x o) m n -> x (o m n)", x=1))
         for ci in range(1, len(CHUNKS)):
-            if bases[ci] < HEAD_TILES * P:
-                load(ci)
+            load(ci)
         identb = const.tile([P, P], BF16, name="identb")
         make_identity(nc, identb[:])
         ident = const.tile([P, P], F32, name="ident")
@@ -221,9 +219,6 @@ def tile_blocklinear_t_kernel(tc, x, weight, bias, out):
             nc.scalar.copy(out=bias_sb[:, h * 512:(h + 1) * 512], in_=bp[:])
 
         for s in range(NT + 1):
-            for ci in range(len(CHUNKS)):
-                if bases[ci] >= HEAD_TILES * P and max(bases[ci] // P - AHEAD, 0) == s:
-                    load(ci)
             if s + G_AHEAD < NT and s + G_AHEAD >= 8 and (s + G_AHEAD) % G_EVERY == 0:
                 permute_gpsimd(s + G_AHEAD)
             if s + 3 < NT and ((s + 3) % G_EVERY != 0 or s + 3 < 8):

@@ -15,8 +15,10 @@ TOKENS = 4096
 NT = TOKENS // P
 FLOPS = 2 * TOKENS * 4 * 512 * 256
 
-CHUNKS = [1, 1, 2, 4, 6, 8, 10]
-UNITS = [1, 1, 2, 4, 6, 8, 4, 3, 2, 1]
+CHUNKS = [1, 1, 1, 1, 2, 2, 4, 4, 4, 4, 4, 4]
+UNITS = [1, 1, 1, 1, 2, 2, 4, 4, 4, 4, 4, 2, 1, 1]
+HEAD_TILES = 16
+AHEAD = 12
 G_EVERY = 2
 G_AHEAD = 6
 G_PIECES = 4
@@ -171,7 +173,8 @@ def tile_blocklinear_t_kernel(tc, x, weight, bias, out):
         load(0)
         nc.sync.dma_start(out=brow[0:1, :], in_=bias.rearrange("(x o) m n -> x (o m n)", x=1))
         for ci in range(1, len(CHUNKS)):
-            load(ci)
+            if bases[ci] < HEAD_TILES * P:
+                load(ci)
         identb = const.tile([P, P], BF16, name="identb")
         make_identity(nc, identb[:])
         ident = const.tile([P, P], F32, name="ident")
@@ -219,6 +222,9 @@ def tile_blocklinear_t_kernel(tc, x, weight, bias, out):
             nc.scalar.copy(out=bias_sb[:, h * 512:(h + 1) * 512], in_=bp[:])
 
         for s in range(NT + 1):
+            for ci in range(len(CHUNKS)):
+                if bases[ci] >= HEAD_TILES * P and bases[ci] // P - AHEAD == s:
+                    load(ci)
             if s + G_AHEAD < NT and s + G_AHEAD >= 8 and (s + G_AHEAD) % G_EVERY == 0:
                 permute_gpsimd(s + G_AHEAD)
             if s + 3 < NT and ((s + 3) % G_EVERY != 0 or s + 3 < 8):

@@ -15,11 +15,12 @@ TOKENS = 4096
 NT = TOKENS // P
 FLOPS = 2 * TOKENS * 4 * 512 * 256
 
-CHUNKS = [1, 1, 1, 1, 2, 2, 4, 4, 4, 4, 4, 4]
-UNITS = [1, 1, 1, 1, 2, 2, 4, 4, 4, 4, 4, 2, 1, 1]
-HEAD_TILES = 16
-AHEAD = 12
-G_EVERY = 2
+GROUP = 8
+LOADS = [1, 1, 1, 1, 2, 2, 4, 4, 8, 8]
+STORES = [4, 4, 8, 4, 4, 2, 2, 2, 1, 1]
+HEAD_TILES = 24
+LAST_LOAD_STEP = 5
+G_OF_7 = (0, 2, 4)
 G_AHEAD = 6
 G_PIECES = 4
 
@@ -28,22 +29,23 @@ def tile_blocklinear_t_kernel(tc, x, weight, bias, out):
     nc = tc.nc
     xf = x.flatten_outer_dims()
     of = out.flatten_outer_dims()
-    assert sum(CHUNKS) == NT and sum(UNITS) == NT
+    assert sum(LOADS) == NT and sum(STORES) == NT
 
-    where = []
-    bases = []
-    base = 0
-    for ci, a_cnt in enumerate(CHUNKS):
-        bases.append(base)
-        for a in range(a_cnt):
-            where.append((ci, a))
-        base += P * a_cnt
+    load_at = []
+    first = 0
+    for cnt in LOADS:
+        assert first // GROUP == (first + cnt - 1) // GROUP
+        load_at.append(first)
+        first += cnt
     unit_of_last = {}
     first = 0
-    for cnt in UNITS:
-        assert where[first][0] == where[first + cnt - 1][0]
+    for cnt in STORES:
+        assert first // GROUP == (first + cnt - 1) // GROUP
         unit_of_last[first + cnt - 1] = cnt
         first += cnt
+
+    def on_gpsimd(n):
+        return n >= 8 and (n - 8) % 7 in G_OF_7
 
     with tc.tile_pool(name="const", bufs=1) as const, \
             tc.tile_pool(name="xin", bufs=1) as xin, \
@@ -58,15 +60,19 @@ def tile_blocklinear_t_kernel(tc, x, weight, bias, out):
         code_tiles = {}
         acc_tiles = {}
 
-        def load(ci):
-            a_cnt = CHUNKS[ci]
-            xt = xin.tile([P, a_cnt * FEAT], BF16, name="xchunk", tag="x%d" % ci)
-            rows = xf[bases[ci]:bases[ci] + P * a_cnt, :]
-            nc.sync.dma_start(out=xt[:], in_=rows.rearrange("(p a) f -> p (a f)", a=a_cnt))
-            x_tiles[ci] = xt
+        def load(li):
+            q, j = divmod(load_at[li], GROUP)
+            cnt = LOADS[li]
+            if j == 0:
+                x_tiles[q] = xin.tile([P, GROUP * FEAT], BF16, name="xgroup", tag="x%d" % q)
+            rows = xf[q * GROUP * P:(q + 1) * GROUP * P, :].rearrange("(p a) f -> p a f", a=GROUP)
+            nc.sync.dma_start(
+                out=x_tiles[q][:, j * FEAT:(j + cnt) * FEAT].rearrange("p (a f) -> p a f", a=cnt),
+                in_=rows[:, j:j + cnt, :],
+            )
 
         def permute_gpsimd(n):
-            ci, a = where[n]
+            ci, a = divmod(n, GROUP)
             xp = work.tile([P, FEAT], BF16, name="xpg", tag="xpg", bufs=3)
             words = x_tiles[ci][:].bitcast(F32)[:, a * (FEAT // 2):(a + 1) * (FEAT // 2)].rearrange(
                 "p (i g k) -> p g i k", g=8, i=16)
@@ -77,7 +83,7 @@ def tile_blocklinear_t_kernel(tc, x, weight, bias, out):
             xp_tiles[n] = xp
 
         def permute(n, on_vector):
-            ci, a = where[n]
+            ci, a = divmod(n, GROUP)
             src = x_tiles[ci]
             xp = work.tile([P, FEAT], BF16, name="xp", tag="xp", bufs=4)
             if on_vector:
@@ -140,10 +146,9 @@ def tile_blocklinear_t_kernel(tc, x, weight, bias, out):
             acc_tiles[n] = accs
 
         def add_bias_and_store(n):
-            ci, a = where[n]
-            a_cnt = CHUNKS[ci]
+            ci, a = divmod(n, GROUP)
             osb = x_tiles[ci][:].bitcast(F32)
-            rows = of[bases[ci]:bases[ci] + P * a_cnt, :].rearrange("(p a) f -> p a f", a=a_cnt)
+            rows = of[ci * GROUP * P:(ci + 1) * GROUP * P, :].rearrange("(p a) f -> p a f", a=GROUP)
             for h in range(2):
                 lo = a * OUTF + h * 512
                 nc.vector.tensor_tensor(
@@ -172,9 +177,9 @@ def tile_blocklinear_t_kernel(tc, x, weight, bias, out):
         )
         load(0)
         nc.sync.dma_start(out=brow[0:1, :], in_=bias.rearrange("(x o) m n -> x (o m n)", x=1))
-        for ci in range(1, len(CHUNKS)):
-            if bases[ci] < HEAD_TILES * P:
-                load(ci)
+        for li in range(1, len(LOADS)):
+            if load_at[li] < HEAD_TILES:
+                load(li)
         identb = const.tile([P, P], BF16, name="identb")
         make_identity(nc, identb[:])
         ident = const.tile([P, P], F32, name="ident")
@@ -222,12 +227,11 @@ def tile_blocklinear_t_kernel(tc, x, weight, bias, out):
             nc.scalar.copy(out=bias_sb[:, h * 512:(h + 1) * 512], in_=bp[:])
 
         for s in range(NT + 1):
-            for ci in range(len(CHUNKS)):
-                if bases[ci] >= HEAD_TILES * P and bases[ci] // P - AHEAD == s:
-                    load(ci)
-            if s + G_AHEAD < NT and s + G_AHEAD >= 8 and (s + G_AHEAD) % G_EVERY == 0:
+            if s == LAST_LOAD_STEP:
+                load(len(LOADS) - 1)
+            if s + G_AHEAD < NT and on_gpsimd(s + G_AHEAD):
                 permute_gpsimd(s + G_AHEAD)
-            if s + 3 < NT and ((s + 3) % G_EVERY != 0 or s + 3 < 8):
+            if s + 3 < NT and not on_gpsimd(s + 3):
                 permute(s + 3, s + 3 in (3, 4))
             if s + 2 < NT:
                 transposes(s + 2)

import concourse.mybir as mybir
from concourse.masks import make_identity

F32 = mybir.dt.float32
BF16 = mybir.dt.bfloat16
U32 = mybir.dt.uint32
U8 = mybir.dt.uint8
FP8X4 = mybir.dt.float8_e4m3fn_x4
ADD = mybir.AluOpType.add

P = 128
FEAT = 2048
OUTF = 1024
TOKENS = 4096
NT = TOKENS // P
FLOPS = 2 * TOKENS * 4 * 512 * 256

GROUP = 8
LOADS = [1, 1, 1, 1, 2, 2, 4, 4, 8, 8]
STORES = [4, 4, 8, 4, 4, 2, 2, 2, 1, 1]
HEAD_TILES = 24
LAST_LOAD_STEP = 5
G_OF_7 = (0, 2, 4)
G_AHEAD = 6
G_PIECES = 4


def tile_blocklinear_t_kernel(tc, x, weight, bias, out):
    nc = tc.nc
    xf = x.flatten_outer_dims()
    of = out.flatten_outer_dims()
    assert sum(LOADS) == NT and sum(STORES) == NT

    load_at = []
    first = 0
    for cnt in LOADS:
        assert first // GROUP == (first + cnt - 1) // GROUP
        load_at.append(first)
        first += cnt
    unit_of_last = {}
    first = 0
    for cnt in STORES:
        assert first // GROUP == (first + cnt - 1) // GROUP
        unit_of_last[first + cnt - 1] = cnt
        first += cnt

    def on_gpsimd(n):
        return n >= 8 and (n - 8) % 7 in G_OF_7

    with tc.tile_pool(name="const", bufs=1) as const, \
            tc.tile_pool(name="xin", bufs=1) as xin, \
            tc.tile_pool(name="work", bufs=3) as work, \
            tc.psum_pool(name="ps", bufs=2) as ps, \
            tc.manual_schedule():

        x_tiles = {}
        xp_tiles = {}
        bank_tiles = {}
        grp_tiles = {}
        code_tiles = {}
        acc_tiles = {}

        def load(li):
            q, j = divmod(load_at[li], GROUP)
            cnt = LOADS[li]
            if j == 0:
                x_tiles[q] = xin.tile([P, GROUP * FEAT], BF16, name="xgroup", tag="x%d" % q)
            rows = xf[q * GROUP * P:(q + 1) * GROUP * P, :].rearrange("(p a) f -> p a f", a=GROUP)
            nc.sync.dma_start(
                out=x_tiles[q][:, j * FEAT:(j + cnt) * FEAT].rearrange("p (a f) -> p a f", a=cnt),
                in_=rows[:, j:j + cnt, :],
            )

        def permute_gpsimd(n):
            ci, a = divmod(n, GROUP)
            xp = work.tile([P, FEAT], BF16, name="xpg", tag="xpg", bufs=3)
            words = x_tiles[ci][:].bitcast(F32)[:, a * (FEAT // 2):(a + 1) * (FEAT // 2)].rearrange(
                "p (i g k) -> p g i k", g=8, i=16)
            sorted_words = xp[:].bitcast(F32).rearrange("p (g i k) -> p g i k", g=8, i=16)
            per = 8 // G_PIECES
            for q in range(G_PIECES):
                nc.gpsimd.tensor_copy(out=sorted_words[:, q * per:(q + 1) * per], in_=words[:, q * per:(q + 1) * per])
            xp_tiles[n] = xp

        def permute(n, on_vector):
            ci, a = divmod(n, GROUP)
            src = x_tiles[ci]
            xp = work.tile([P, FEAT], BF16, name="xp", tag="xp", bufs=4)
            if on_vector:
                nc.vector.tensor_copy(
                    out=xp[:].rearrange("p (g i k) -> p g i k", g=8, i=16),
                    in_=src[:, a * FEAT:(a + 1) * FEAT].rearrange("p (i g k) -> p g i k", g=8, i=16),
                )
            else:
                nc.scalar.copy(
                    out=xp[:].bitcast(F32).rearrange("p (g i k) -> p g i k", g=8, i=16),
                    in_=src[:].bitcast(F32)[:, a * (FEAT // 2):(a + 1) * (FEAT // 2)].rearrange(
                        "p (i g k) -> p g i k", g=8, i=16),
                )
            xp_tiles[n] = xp

        def transposes(n):
            xpw = xp_tiles[n][:].bitcast(F32)
            banks = []
            for h in range(2):
                bank = ps.tile([P, 2, 2, P], F32, name="xt%d" % h, tag="xt%d" % h)
                for ml in range(2):
                    for u in range(2):
                        g = 4 * u + 2 * h + ml
                        nc.tensor.transpose(bank[:, ml, u, :], xpw[:, g * P:(g + 1) * P], ident[:])
                banks.append(bank)
            bank_tiles[n] = banks

        def copy_out(n):
            grp = work.tile([P, FEAT], BF16, name="grp", tag="grp", align_bytes=64)
            gw = grp[:].bitcast(F32)
            for h in range(2):
                nc.scalar.copy(
                    out=gw[:, h * 512:(h + 1) * 512].rearrange("p (m r u) -> p m r u", m=2, u=2),
                    in_=bank_tiles[n][h][:].rearrange("p m u r -> p m r u"),
                )
            grp_tiles[n] = grp

        def quantise(n):
            codes = work.tile([P, 512], U32, name="codes", tag="codes", align_bytes=64)
            scl = work.tile([P, 512], U8, name="scl", tag="scl", align_bytes=64)
            nc.vector.quantize_mx(out=codes[:].bitcast(FP8X4), scales=scl[:], in_=grp_tiles[n][:])
            code_tiles[n] = (codes, scl)

        def multiply(n):
            codes, scl = code_tiles[n]
            accs = []
            for h in range(2):
                acc = ps.tile([P, 512], F32, name="acc%d" % h, tag="acc%d" % h)
                for m in range(4):
                    nc.tensor.matmul_mx(
                        out=acc[:, m * P:(m + 1) * P],
                        lhsT=codes[:, m * P:(m + 1) * P].bitcast(FP8X4),
                        lhsT_scale=scl[:, m * P:(m + 1) * P],
                        rhs=wcodes[:, h * P:(h + 1) * P].bitcast(FP8X4),
                        rhs_scale=wscl[:, h * P:(h + 1) * P],
                        start=True,
                        stop=True,
                    )
                accs.append(acc)
            acc_tiles[n] = accs

        def add_bias_and_store(n):
            ci, a = divmod(n, GROUP)
            osb = x_tiles[ci][:].bitcast(F32)
            rows = of[ci * GROUP * P:(ci + 1) * GROUP * P, :].rearrange("(p a) f -> p a f", a=GROUP)
            for h in range(2):
                lo = a * OUTF + h * 512
                nc.vector.tensor_tensor(
                    out=osb[:, lo:lo + 512].rearrange("p (o m n) -> p o m n", o=4, m=4),
                    in0=acc_tiles[n][h][:].rearrange("p (m o n) -> p o m n", m=4, o=4),
                    in1=bias_sb[:, h * 512:(h + 1) * 512].rearrange("p (o m n) -> p o m n", o=4, m=4),
                    op=ADD,
                )
                if n == NT - 1:
                    nc.sync.dma_start(out=rows[:, a, h * 512:(h + 1) * 512], in_=osb[:, lo:lo + 512])
            if n in unit_of_last and n < NT - 1:
                cnt = unit_of_last[n]
                nc.sync.dma_start(
                    out=rows[:, a - cnt + 1:a + 1, :],
                    in_=osb[:, (a - cnt + 1) * OUTF:(a + 1) * OUTF].rearrange("p (a f) -> p a f", a=cnt),
                )

        brow = const.tile([P, OUTF], BF16, name="brow")
        nc.vector.memset(brow[:], 0.0)
        ones = const.tile([P, P], BF16, name="ones")
        nc.vector.memset(ones[:], 1.0)
        wa = const.tile([P, 1024], BF16, name="wa")
        nc.sync.dma_start(
            out=wa[:].rearrange("p (ol q) -> p ol q", ol=2),
            in_=weight.rearrange("(ol oh) c n k -> (oh c) ol (n k)", ol=2),
        )
        load(0)
        nc.sync.dma_start(out=brow[0:1, :], in_=bias.rearrange("(x o) m n -> x (o m n)", x=1))
        for li in range(1, len(LOADS)):
            if load_at[li] < HEAD_TILES:
                load(li)
        identb = const.tile([P, P], BF16, name="identb")
        make_identity(nc, identb[:])
        ident = const.tile([P, P], F32, name="ident")
        make_identity(nc, ident[:])

        wb = const.tile([P, 1024], BF16, name="wb")
        nc.vector.tensor_copy(
            out=wb[:].bitcast(F32).rearrange("p (k q) -> p k q", k=8),
            in_=wa[:].bitcast(F32).rearrange("p (q k) -> p k q", k=8),
        )
        y_ps = ps.tile([P, 1024], BF16, name="y_ps", tag="acc0")
        for k2 in range(8):
            nc.tensor.transpose(y_ps[:, k2 * P:(k2 + 1) * P], wb[:, k2 * P:(k2 + 1) * P], identb[:])
        y_sb = const.tile([P, 1024], BF16, name="y_sb")
        ysv = y_sb[:].rearrange("p (oh u i k) -> p u oh i k", oh=4, u=2, i=16)
        ypv = y_ps[:].rearrange("p (k oh i u) -> p u oh i k", k=8, oh=4, i=16)
        for u in range(2):
            nc.scalar.copy(out=ysv[:, u], in_=ypv[:, u])

        permute(0, True)
        transposes(0)
        copy_out(0)

        z_ps = ps.tile([P, 1024], BF16, name="z_ps", tag="acc1")
        for q in range(8):
            nc.tensor.transpose(z_ps[:, q * P:(q + 1) * P], y_sb[:, q * P:(q + 1) * P], identb[:])
        wgrp = const.tile([P, 1024], BF16, name="wgrp", align_bytes=64)
        wgv = wgrp[:].bitcast(F32).rearrange("p (ol oh n u) -> p ol oh n u", ol=2, oh=4, u=2)
        zv = z_ps[:].bitcast(F32).rearrange("p (oh u ol n) -> p ol oh n u", oh=4, u=2, ol=2)
        for ol in range(2):
            nc.scalar.copy(out=wgv[:, ol], in_=zv[:, ol])
        wcodes = const.tile([P, 256], U32, name="wcodes", align_bytes=64)
        wscl = const.tile([P, 256], U8, name="wscl", align_bytes=64)

        permute(1, True)
        transposes(1)
        permute(2, True)
        nc.vector.quantize_mx(out=wcodes[:].bitcast(FP8X4), scales=wscl[:], in_=wgrp[:])
        copy_out(1)
        quantise(0)
        bias_sb = const.tile([P, OUTF], F32, name="bias_sb")
        for h in range(2):
            bp = ps.tile([P, 512], F32, name="bp%d" % h, tag="acc%d" % h)
            nc.tensor.matmul(bp[:], lhsT=ones[:], rhs=brow[:, h * 512:(h + 1) * 512], start=True, stop=True)
            nc.scalar.copy(out=bias_sb[:, h * 512:(h + 1) * 512], in_=bp[:])

        for s in range(NT + 1):
            if s == LAST_LOAD_STEP:
                load(len(LOADS) - 1)
            if s + G_AHEAD < NT and on_gpsimd(s + G_AHEAD):
                permute_gpsimd(s + G_AHEAD)
            if s + 3 < NT and not on_gpsimd(s + 3):
                permute(s + 3, s + 3 in (3, 4))
            if s + 2 < NT:
                transposes(s + 2)
                copy_out(s + 2)
            if s >= 1:
                add_bias_and_store(s - 1)
            if s < NT:
                multiply(s)
            if s + 1 < NT:
                quantise(s + 1)
